import numpy as np
import ml_dtypes


def mxq(x, axis, fmt="e4m3"):
    dtype, down = {"e4m3": (ml_dtypes.float8_e4m3fn, 7), "e5m2": (ml_dtypes.float8_e5m2, 14)}[fmt]
    v = np.moveaxis(np.asarray(x, np.float32).astype(ml_dtypes.bfloat16).astype(np.float64), axis, -1)
    blocks = v.reshape(v.shape[:-1] + (-1, 32))
    amax = np.abs(blocks).max(-1, keepdims=True)
    byte = np.maximum(np.where(amax > 0, np.frexp(amax)[1] - 1 + 127, 0) - down, 1)
    scale = np.exp2(byte - 127.0)
    codes = (blocks / scale).astype(np.float32).astype(dtype).astype(np.float64)
    return np.moveaxis((codes * scale).reshape(v.shape), -1, axis)


WIDE = False


def mx_kscale(k):
    if not WIDE:
        return np.ones(k)
    levels = np.array([10, -10, 5, -5, 0])
    if k % 512:
        return np.exp2(np.random.permutation(np.resize(levels, k // 32))).repeat(32)
    a = np.empty((k // 512, 16))
    for p in range(k // 512):
        a[p, :8] = np.random.permutation(np.resize(levels, 8))
        for g in range(8):
            far = levels[np.abs(levels - a[p, g]) >= 10]
            a[p, g + 8] = far[np.random.randint(len(far))]
    return np.exp2(a.ravel()).repeat(32)


BF16 = ml_dtypes.bfloat16


def bf(x):
    return np.asarray(x, np.float32).astype(BF16)


def f64(x):
    return np.asarray(x).astype(np.float64)


B, C, HH, WW = 1, 2048, 64, 64
N = HH * WW


def setup_inputs():
    s, t = mx_kscale(C), mx_kscale(C)
    return {"x": bf(np.random.standard_normal((B, C, HH, WW)) * s[None, :, None, None]),
            "Wq": bf(np.random.standard_normal((C, C)) * 1.4 / np.sqrt(C) * t[:, None] / s[None, :]),
            "bq": bf(np.random.standard_normal(C) * 0.2 * t),
            "k": bf(np.random.standard_normal((B, N, C)) * 1.4 / t)}


def reference(x, Wq, bq, k):
    xt = f64(x).reshape(B, C, N)
    q = (mxq(xt, 1, "e4m3").transpose(0, 2, 1) @ mxq(f64(Wq), 1, "e4m3").T) + f64(bq)
    scores = mxq(q / np.sqrt(C), 2, "e4m3") @ mxq(f64(k), 2, "e4m3").transpose(0, 2, 1)
    e = np.exp(scores - scores.max(-1, keepdims=True))
    return e / e.sum(-1, keepdims=True)

@@ -1,0 +1,330 @@
+import math
+from contextlib import ExitStack
+
+import concourse.mybir as mybir
+from concourse.masks import make_identity
+
+C = 2048
+TOKENS = 4096
+KEYS = 4096
+FLOPS = 2 * TOKENS * C * C + 2 * TOKENS * KEYS * C
+
+F32 = mybir.dt.float32
+BF16 = mybir.dt.bfloat16
+U32 = mybir.dt.uint32
+U8 = mybir.dt.uint8
+FP8X4 = mybir.dt.float8_e4m3fn_x4
+ALU = mybir.AluOpType
+ACT = mybir.ActivationFunctionType
+AX = mybir.AxisListType
+
+P = 128
+PACK = 4
+PASSES = C // (P * PACK)
+WIDE = 512
+
+CHUNKS = TOKENS // WIDE
+GROUPS = C // WIDE
+BLOCKS = CHUNKS * GROUPS
+W_UNITS = C // P
+UNITS = W_UNITS + KEYS // P
+RUNS = UNITS // 2
+X_LEAD = 6
+ROW_TILES = TOKENS // P
+KEY_CHUNKS = KEYS // WIDE
+POOL_COLS = 2560
+
+
+def plane(tile_ap, g, cols):
+    return tile_ap[PACK * g : P, cols]
+
+
+def project_queries(tc, keep, psum, pool, x_rows, w_rows, k_rows, bq_cols, k_codes, k_planes, x_codes, q_codes, q_planes):
+    nc = tc.nc
+    inv_sqrt_c = 1.0 / math.sqrt(C)
+
+    raws, banks, turned = {}, {}, {}
+    x_raws, x_grouped, x_planes = {}, {}, {}
+    accs, q_rows, q_grouped = {}, {}, {}
+
+    w_codes = [pool.tile([P, PASSES, P], U32, name="w_codes%d" % r, align_bytes=64) for r in range(W_UNITS)]
+    w_planes = [pool.tile([P, P], U8, name="w_planes%d" % r, align_bytes=64) for r in range(W_UNITS)]
+    ident = pool.tile([P, P], F32, name="ident")
+    warm = pool.tile([P, 1], F32, name="warm")
+    bq_raw = pool.tile([P, GROUPS, PACK], BF16, name="bq_raw")
+    bias = pool.tile([P, W_UNITS], F32, name="bias")
+    x_codes[CHUNKS - 1] = pool.tile([P, PASSES, WIDE], U32, name="x_last", align_bytes=64)
+
+    def load_unit(u):
+        if u >= UNITS:
+            return
+        raw = pool.tile([P, C], BF16, name="raw", tag="raw", bufs=4)
+        rows = w_rows[u // PACK, u % PACK] if u < W_UNITS else k_rows[u - W_UNITS]
+        nc.sync.dma_start(out=raw[:], in_=rows)
+        raws[u] = raw
+
+    def transpose_run(run):
+        for u in (2 * run, 2 * run + 1):
+            words = raws[u][:].bitcast(F32)
+            for h in range(2):
+                bank = psum.tile([P, WIDE], F32, name="tr", tag="tr")
+                view = bank[:].rearrange("p (a e r) -> p a e r", a=2, e=2)
+                for a in range(2):
+                    g = 2 * h + a
+                    for e in range(2):
+                        nc.tensor.transpose(view[:, a, e, :], words[:, 256 * g + e : 256 * (g + 1) : 2], ident[:])
+                banks[(u, h)] = bank
+        load_unit(2 * run + 4)
+        load_unit(2 * run + 5)
+
+    def copy_run(run):
+        for u in (2 * run, 2 * run + 1):
+            grouped = pool.tile([P, PASSES, P, PACK], BF16, name="kg", tag="kg", bufs=2, align_bytes=64)
+            for h in range(2):
+                nc.scalar.copy(
+                    out=grouped[:].bitcast(F32)[:, 2 * h : 2 * h + 2],
+                    in_=banks[(u, h)][:].rearrange("p (a e r) -> p a r e", a=2, e=2),
+                )
+            turned[u] = grouped
+
+    def quantize_unit(u):
+        if u < W_UNITS:
+            codes, planes, c0 = w_codes[u], w_planes[u], 0
+        else:
+            v = u - W_UNITS
+            codes, planes, c0 = k_codes[v // PACK], k_planes[v // PACK], P * (v % PACK)
+        cols = slice(c0, c0 + P)
+        for g in range(PASSES):
+            nc.vector.quantize_mx(
+                out=codes[:, g, cols].bitcast(FP8X4),
+                scales=plane(planes, g, cols),
+                in_=turned[u][:, g].rearrange("p r j -> p (r j)"),
+            )
+
+    def load_x(xu):
+        if xu >= BLOCKS:
+            return
+        i, g = divmod(xu, PASSES)
+        raw = pool.tile([P, PACK, WIDE], BF16, name="xraw", tag="xraw", bufs=3)
+        nc.sync.dma_start(out=raw[:], in_=x_rows[g, :, :, WIDE * i : WIDE * (i + 1)])
+        x_raws[xu] = raw
+
+    def interleave_x(xu):
+        grouped = pool.tile([P, WIDE, PACK], BF16, name="grp", tag="grp", bufs=3, align_bytes=64)
+        nc.vector.tensor_copy(out=grouped[:], in_=x_raws[xu][:].rearrange("p j n -> p n j"))
+        x_grouped[xu] = grouped
+        load_x(xu + 3)
+
+    def quantize_x(xu):
+        i, g = divmod(xu, PASSES)
+        if g == 0:
+            x_planes[i] = pool.tile([P, WIDE], U8, name="xp", tag="xp", bufs=3, align_bytes=64)
+        nc.vector.quantize_mx(
+            out=x_codes[i][:, g, :].bitcast(FP8X4),
+            scales=plane(x_planes[i], g, slice(0, WIDE)),
+            in_=x_grouped[xu][:].rearrange("p n j -> p (n j)"),
+        )
+
+    def project_half(n, half):
+        i, a = divmod(n, GROUPS)
+        for t in (2 * half, 2 * half + 1):
+            r = PACK * a + t
+            acc = psum.tile([P, WIDE], F32, name="acc", tag="acc")
+            for g in range(PASSES):
+                nc.tensor.matmul_mx(
+                    out=acc[:],
+                    lhsT=w_codes[r][:, g, :].bitcast(FP8X4),
+                    lhsT_scale=plane(w_planes[r], g, slice(0, P)),
+                    rhs=x_codes[i][:, g, :].bitcast(FP8X4),
+                    rhs_scale=plane(x_planes[i], g, slice(0, WIDE)),
+                    start=(g == 0),
+                    stop=(g == PASSES - 1),
+                )
+            accs[(n, t)] = acc
+
+    def evacuate_half(n, half):
+        a = n % GROUPS
+        if half == 0:
+            q_rows[n] = pool.tile([P, PACK, WIDE], BF16, name="qbf", tag="qbf", bufs=2)
+        for t in (2 * half, 2 * half + 1):
+            r = PACK * a + t
+            nc.scalar.activation(
+                out=q_rows[n][:, t, :], in_=accs[(n, t)][:], func=ACT.Identity, bias=bias[:, r : r + 1], scale=inv_sqrt_c
+            )
+
+    def interleave_q(n):
+        grouped = pool.tile([P, WIDE, PACK], BF16, name="grp", tag="grp", bufs=3, align_bytes=64)
+        nc.vector.tensor_copy(out=grouped[:], in_=q_rows[n][:].rearrange("p t n -> p n t"))
+        q_grouped[n] = grouped
+
+    def quantize_q(n):
+        i, a = divmod(n, GROUPS)
+        if a == 0 and i > 0:
+            q_codes[i] = keep.tile([P, PASSES, WIDE], U32, name="slot%d" % i, tag="slot%d" % i, align_bytes=64)
+        nc.vector.quantize_mx(
+            out=q_codes[i][:, a, :].bitcast(FP8X4),
+            scales=plane(q_planes[i], a, slice(0, WIDE)),
+            in_=q_grouped[n][:].rearrange("p n j -> p (n j)"),
+        )
+
+    for xu in range(3):
+        load_x(xu)
+    for u in range(4):
+        load_unit(u)
+    nc.sync.dma_start(out=bq_raw[:], in_=bq_cols)
+    nc.vector.memset(warm[:], 0.0)
+    nc.scalar.activation(out=warm[:], in_=warm[:], func=ACT.Exp)
+    make_identity(nc, ident[:])
+
+    interleave_x(0)
+    interleave_x(1)
+    quantize_x(0)
+    interleave_x(2)
+    quantize_x(1)
+    nc.vector.tensor_scalar(
+        out=bias[:], in0=bq_raw[:].rearrange("p a t -> p (a t)"), scalar1=inv_sqrt_c, scalar2=None, op0=ALU.mult
+    )
+    quantize_x(2)
+    transpose_run(0)
+    copy_run(0)
+    quantize_unit(0)
+    interleave_x(3)
+    quantize_unit(1)
+    quantize_x(3)
+
+    for h in range(2 * GROUPS):
+        transpose_run(h + 1)
+        copy_run(h + 1)
+        project_half(h // 2, h % 2)
+        evacuate_half(h // 2, h % 2)
+        xu = PASSES + h
+        if xu < PASSES + X_LEAD:
+            interleave_x(xu)
+        quantize_unit(2 * h + 2)
+        if h % 2 == 0 and h >= 2:
+            interleave_q(h // 2 - 1)
+        quantize_unit(2 * h + 3)
+        if xu < PASSES + X_LEAD:
+            quantize_x(xu)
+        if h % 2 == 0 and h >= 2:
+            quantize_q(h // 2 - 1)
+
+    first_k_run = 2 * GROUPS + 1
+    run_after = {}
+    for j in range(RUNS - first_k_run):
+        run_after[GROUPS + 17 * j // 10] = first_k_run + j
+    waiting = []
+    for n in range(GROUPS, BLOCKS):
+        project_half(n, 0)
+        evacuate_half(n, 0)
+        project_half(n, 1)
+        evacuate_half(n, 1)
+        xu = n + X_LEAD
+        if xu < BLOCKS:
+            interleave_x(xu)
+        interleave_q(n - 1)
+        if xu < BLOCKS:
+            quantize_x(xu)
+        for u in waiting:
+            quantize_unit(u)
+        quantize_q(n - 1)
+        waiting = []
+        if n in run_after:
+            transpose_run(run_after[n])
+            copy_run(run_after[n])
+            waiting = [2 * run_after[n], 2 * run_after[n] + 1]
+    interleave_q(BLOCKS - 1)
+    for u in waiting:
+        quantize_unit(u)
+    quantize_q(BLOCKS - 1)
+
+
+def attention_rows(tc, psum, pool, q_codes, q_planes, k_codes, k_planes, out_rows):
+    nc = tc.nc
+    banks, negs, lows, shifts, totals = {}, {}, {}, {}, {}
+
+    def scores(r):
+        i, s = divmod(r, WIDE // P)
+        cols = slice(P * s, P * (s + 1))
+        for b in range(KEY_CHUNKS):
+            bank = psum.tile([P, WIDE], F32, name="sc", tag=("acc", "tr")[b % 2])
+            for g in range(PASSES):
+                nc.tensor.matmul_mx(
+                    out=bank[:],
+                    lhsT=q_codes[i][:, g, cols].bitcast(FP8X4),
+                    lhsT_scale=plane(q_planes[i], g, cols),
+                    rhs=k_codes[b][:, g, :].bitcast(FP8X4),
+                    rhs_scale=plane(k_planes[b], g, slice(0, WIDE)),
+                    start=(g == 0),
+                    stop=(g == PASSES - 1),
+                )
+            banks[(r, b)] = bank
+
+    def drain(r, b):
+        if b == 0:
+            negs[r] = pool.tile([P, KEYS], F32, name="neg", tag="neg", bufs=4)
+            lows[r] = pool.tile([P, KEY_CHUNKS], F32, name="low", tag="low", bufs=3)
+        nc.vector.tensor_scalar(
+            out=negs[r][:, WIDE * b : WIDE * (b + 1)],
+            in0=banks[(r, b)][:],
+            scalar1=-1.0,
+            scalar2=None,
+            op0=ALU.mult,
+            op1=ALU.min,
+            accum_out=lows[r][:, b : b + 1],
+        )
+
+    def exponent(r):
+        shifts[r] = pool.tile([P, 1], F32, name="shift", tag="shift", bufs=3)
+        totals[r] = pool.tile([P, 1], F32, name="total", tag="total", bufs=3)
+        nc.vector.tensor_reduce(out=shifts[r][:], in_=lows[r][:], axis=AX.X, op=ALU.min)
+        nc.scalar.activation(
+            out=negs[r][:], in_=negs[r][:], func=ACT.Exp, bias=shifts[r][:, 0:1], scale=-1.0, accum_out=totals[r][:, 0:1]
+        )
+
+    def normalise(r):
+        inv = pool.tile([P, 1], F32, name="inv", tag="inv", bufs=3)
+        nc.vector.reciprocal(out=inv[:], in_=totals[r][:])
+        left = negs[r][:, :POOL_COLS]
+        right = negs[r][:, POOL_COLS:]
+        nc.gpsimd.tensor_scalar(out=left, in0=left, scalar1=inv[:, 0:1], scalar2=0.0, op0=ALU.mult, op1=ALU.add)
+        nc.scalar.activation(out=right, in_=right, func=ACT.Copy, scale=inv[:, 0:1])
+        nc.sync.dma_start(out=out_rows[r, :, POOL_COLS:], in_=right)
+        nc.sync.dma_start(out=out_rows[r, :, :POOL_COLS], in_=left)
+
+    for r in range(ROW_TILES):
+        scores(r)
+        for b in range(KEY_CHUNKS // 2):
+            drain(r, b)
+        if r > 0:
+            normalise(r - 1)
+        for b in range(KEY_CHUNKS // 2, KEY_CHUNKS):
+            drain(r, b)
+        exponent(r)
+    normalise(ROW_TILES - 1)
+
+
+def tile_visionattention_pa_l_kernel(tc, x, Wq, bq, k, out):
+    x_rows = x[0].rearrange("(g p j) h w -> g p j (h w)", p=P, j=PACK)
+    w_rows = Wq.rearrange("(a m t) c -> a t m c", m=P, t=PACK)
+    k_rows = k[0].rearrange("(u p) c -> u p c", p=P)
+    bq_cols = bq.rearrange("(a m t) -> m a t", m=P, t=PACK)
+    out_rows = out[0].rearrange("(r p) m -> r p m", p=P)
+
+    with ExitStack() as ctx:
+        ctx.enter_context(tc.manual_schedule())
+        keep = ctx.enter_context(tc.tile_pool(name="keep", bufs=1))
+        psum = ctx.enter_context(tc.psum_pool(name="psum", bufs=4))
+
+        k_codes = [keep.tile([P, PASSES, WIDE], U32, name="k_codes%d" % b, align_bytes=64) for b in range(KEY_CHUNKS)]
+        k_planes = [keep.tile([P, WIDE], U8, name="k_planes%d" % b, align_bytes=64) for b in range(KEY_CHUNKS)]
+        q_planes = [keep.tile([P, WIDE], U8, name="q_planes%d" % i, align_bytes=64) for i in range(CHUNKS)]
+        q_codes = {0: keep.tile([P, PASSES, WIDE], U32, name="slot0", tag="slot0", align_bytes=64)}
+        x_codes = {}
+        for i in range(CHUNKS - 1):
+            x_codes[i] = keep.tile([P, PASSES, WIDE], U32, name="slot%d" % (i + 1), tag="slot%d" % (i + 1), align_bytes=64)
+
+        with tc.tile_pool(name="first", bufs=1) as first:
+            project_queries(tc, keep, psum, first, x_rows, w_rows, k_rows, bq_cols, k_codes, k_planes, x_codes, q_codes, q_planes)
+        with tc.tile_pool(name="second", bufs=1) as second:
+            attention_rows(tc, psum, second, q_codes, q_planes, k_codes, k_planes, out_rows)

@@ -30,9 +30,12 @@ W_UNITS = C // P
 UNITS = W_UNITS + KEYS // P
 RUNS = UNITS // 2
 X_LEAD = 6
+X_SPLIT = 256
+GRP_BUFS = 2
+QBF_BUFS = 3
 ROW_TILES = TOKENS // P
 KEY_CHUNKS = KEYS // WIDE
-POOL_COLS = 2560
+LEFT_BANKS = 5
 
 
 def plane(tile_ap, g, cols):
@@ -109,9 +112,13 @@ def project_queries(tc, keep, psum, pool, x_rows, w_rows, k_rows, bq_cols, k_cod
         nc.sync.dma_start(out=raw[:], in_=x_rows[g, :, :, WIDE * i : WIDE * (i + 1)])
         x_raws[xu] = raw
 
-    def interleave_x(xu):
-        grouped = pool.tile([P, WIDE, PACK], BF16, name="grp", tag="grp", bufs=3, align_bytes=64)
-        nc.vector.tensor_copy(out=grouped[:], in_=x_raws[xu][:].rearrange("p j n -> p n j"))
+    def interleave_x(xu, shared):
+        grouped = pool.tile([P, WIDE, PACK], BF16, name="grp", tag="grp", bufs=GRP_BUFS, align_bytes=64)
+        turned_x = x_raws[xu][:].rearrange("p j n -> p n j")
+        split = X_SPLIT if shared else WIDE
+        nc.vector.tensor_copy(out=grouped[:, :split, :], in_=turned_x[:, :split, :])
+        if shared:
+            nc.scalar.copy(out=grouped[:, split:, :], in_=turned_x[:, split:, :])
         x_grouped[xu] = grouped
         load_x(xu + 3)
 
@@ -145,7 +152,7 @@ def project_queries(tc, keep, psum, pool, x_rows, w_rows, k_rows, bq_cols, k_cod
     def evacuate_half(n, half):
         a = n % GROUPS
         if half == 0:
-            q_rows[n] = pool.tile([P, PACK, WIDE], BF16, name="qbf", tag="qbf", bufs=2)
+            q_rows[n] = pool.tile([P, PACK, WIDE], BF16, name="qbf", tag="qbf", bufs=QBF_BUFS)
         for t in (2 * half, 2 * half + 1):
             r = PACK * a + t
             nc.scalar.activation(
@@ -153,7 +160,7 @@ def project_queries(tc, keep, psum, pool, x_rows, w_rows, k_rows, bq_cols, k_cod
             )
 
     def interleave_q(n):
-        grouped = pool.tile([P, WIDE, PACK], BF16, name="grp", tag="grp", bufs=3, align_bytes=64)
+        grouped = pool.tile([P, WIDE, PACK], BF16, name="grp", tag="grp", bufs=GRP_BUFS, align_bytes=64)
         nc.vector.tensor_copy(out=grouped[:], in_=q_rows[n][:].rearrange("p t n -> p n t"))
         q_grouped[n] = grouped
 
@@ -176,10 +183,10 @@ def project_queries(tc, keep, psum, pool, x_rows, w_rows, k_rows, bq_cols, k_cod
     nc.scalar.activation(out=warm[:], in_=warm[:], func=ACT.Exp)
     make_identity(nc, ident[:])
 
-    interleave_x(0)
-    interleave_x(1)
+    interleave_x(0, True)
+    interleave_x(1, True)
     quantize_x(0)
-    interleave_x(2)
+    interleave_x(2, True)
     quantize_x(1)
     nc.vector.tensor_scalar(
         out=bias[:], in0=bq_raw[:].rearrange("p a t -> p (a t)"), scalar1=inv_sqrt_c, scalar2=None, op0=ALU.mult
@@ -188,7 +195,7 @@ def project_queries(tc, keep, psum, pool, x_rows, w_rows, k_rows, bq_cols, k_cod
     transpose_run(0)
     copy_run(0)
     quantize_unit(0)
-    interleave_x(3)
+    interleave_x(3, True)
     quantize_unit(1)
     quantize_x(3)
 
@@ -199,7 +206,7 @@ def project_queries(tc, keep, psum, pool, x_rows, w_rows, k_rows, bq_cols, k_cod
         evacuate_half(h // 2, h % 2)
         xu = PASSES + h
         if xu < PASSES + X_LEAD:
-            interleave_x(xu)
+            interleave_x(xu, False)
         quantize_unit(2 * h + 2)
         if h % 2 == 0 and h >= 2:
             interleave_q(h // 2 - 1)
@@ -209,11 +216,13 @@ def project_queries(tc, keep, psum, pool, x_rows, w_rows, k_rows, bq_cols, k_cod
         if h % 2 == 0 and h >= 2:
             quantize_q(h // 2 - 1)
 
-    first_k_run = 2 * GROUPS + 1
+    transpose_run(2 * GROUPS + 1)
+    copy_run(2 * GROUPS + 1)
+    waiting = [4 * GROUPS + 2, 4 * GROUPS + 3]
+    first_k_run = 2 * GROUPS + 2
     run_after = {}
     for j in range(RUNS - first_k_run):
-        run_after[GROUPS + 17 * j // 10] = first_k_run + j
-    waiting = []
+        run_after[GROUPS + 2 * j] = first_k_run + j
     for n in range(GROUPS, BLOCKS):
         project_half(n, 0)
         evacuate_half(n, 0)
@@ -221,7 +230,7 @@ def project_queries(tc, keep, psum, pool, x_rows, w_rows, k_rows, bq_cols, k_cod
         evacuate_half(n, 1)
         xu = n + X_LEAD
         if xu < BLOCKS:
-            interleave_x(xu)
+            interleave_x(xu, n in run_after)
         interleave_q(n - 1)
         if xu < BLOCKS:
             quantize_x(xu)
@@ -241,7 +250,10 @@ def project_queries(tc, keep, psum, pool, x_rows, w_rows, k_rows, bq_cols, k_cod
 
 def attention_rows(tc, psum, pool, q_codes, q_planes, k_codes, k_planes, out_rows):
     nc = tc.nc
-    banks, negs, lows, shifts, totals = {}, {}, {}, {}, {}
+    banks, negs, lows, sums, shifts, weights, factors = {}, {}, {}, {}, {}, {}, {}
+
+    def bank_cols(b):
+        return slice(WIDE * b, WIDE * (b + 1))
 
     def scores(r):
         i, s = divmod(r, WIDE // P)
@@ -260,48 +272,71 @@ def attention_rows(tc, psum, pool, q_codes, q_planes, k_codes, k_planes, out_row
                 )
             banks[(r, b)] = bank
 
-    def drain(r, b):
+    def exponent(r, b):
         if b == 0:
             negs[r] = pool.tile([P, KEYS], F32, name="neg", tag="neg", bufs=4)
             lows[r] = pool.tile([P, KEY_CHUNKS], F32, name="low", tag="low", bufs=3)
+            sums[r] = pool.tile([P, KEY_CHUNKS], F32, name="sums", tag="sums", bufs=3)
+        part = negs[r][:, bank_cols(b)]
         nc.vector.tensor_scalar(
-            out=negs[r][:, WIDE * b : WIDE * (b + 1)],
-            in0=banks[(r, b)][:],
-            scalar1=-1.0,
-            scalar2=None,
-            op0=ALU.mult,
-            op1=ALU.min,
-            accum_out=lows[r][:, b : b + 1],
+            out=part, in0=banks[(r, b)][:], scalar1=-1.0, scalar2=None, op0=ALU.mult, op1=ALU.min, accum_out=lows[r][:, b : b + 1]
         )
-
-    def exponent(r):
-        shifts[r] = pool.tile([P, 1], F32, name="shift", tag="shift", bufs=3)
-        totals[r] = pool.tile([P, 1], F32, name="total", tag="total", bufs=3)
-        nc.vector.tensor_reduce(out=shifts[r][:], in_=lows[r][:], axis=AX.X, op=ALU.min)
         nc.scalar.activation(
-            out=negs[r][:], in_=negs[r][:], func=ACT.Exp, bias=shifts[r][:, 0:1], scale=-1.0, accum_out=totals[r][:, 0:1]
+            out=part, in_=part, func=ACT.Exp, bias=lows[r][:, b : b + 1], scale=-1.0, accum_out=sums[r][:, b : b + 1]
         )
 
-    def normalise(r):
+    def bank_weights(r):
+        shifts[r] = pool.tile([P, 1], F32, name="shift", tag="shift", bufs=3)
+        weights[r] = pool.tile([P, KEY_CHUNKS], F32, name="weight", tag="weight", bufs=3)
+        nc.vector.tensor_reduce(out=shifts[r][:], in_=lows[r][:], axis=AX.X, op=ALU.min)
+        nc.scalar.activation(out=weights[r][:], in_=lows[r][:], func=ACT.Exp, bias=shifts[r][:, 0:1], scale=-1.0)
+
+    def bank_factors(r):
+        weighted = pool.tile([P, KEY_CHUNKS], F32, name="weighted", tag="weighted", bufs=3)
+        total = pool.tile([P, 1], F32, name="total", tag="total", bufs=3)
         inv = pool.tile([P, 1], F32, name="inv", tag="inv", bufs=3)
-        nc.vector.reciprocal(out=inv[:], in_=totals[r][:])
-        left = negs[r][:, :POOL_COLS]
-        right = negs[r][:, POOL_COLS:]
-        nc.gpsimd.tensor_scalar(out=left, in0=left, scalar1=inv[:, 0:1], scalar2=0.0, op0=ALU.mult, op1=ALU.add)
-        nc.scalar.activation(out=right, in_=right, func=ACT.Copy, scale=inv[:, 0:1])
-        nc.sync.dma_start(out=out_rows[r, :, POOL_COLS:], in_=right)
-        nc.sync.dma_start(out=out_rows[r, :, :POOL_COLS], in_=left)
+        factors[r] = pool.tile([P, KEY_CHUNKS], F32, name="factor", tag="factor", bufs=3)
+        nc.vector.scalar_tensor_tensor(
+            out=weighted[:], in0=weights[r][:], scalar=1.0, in1=sums[r][:], op0=ALU.mult, op1=ALU.mult, accum_out=total[:, 0:1]
+        )
+        nc.vector.reciprocal(out=inv[:], in_=total[:])
+        nc.vector.tensor_scalar(out=factors[r][:], in0=weights[r][:], scalar1=inv[:, 0:1], scalar2=None, op0=ALU.mult)
+
+    def scale_left(r, b):
+        engine = nc.vector if r == ROW_TILES - 1 else nc.gpsimd
+        part = negs[r][:, bank_cols(b)]
+        engine.tensor_scalar(out=part, in0=part, scalar1=factors[r][:, b : b + 1], scalar2=0.0, op0=ALU.mult, op1=ALU.add)
+
+    def scale_right(r, b):
+        part = negs[r][:, bank_cols(b)]
+        nc.scalar.activation(out=part, in_=part, func=ACT.Copy, scale=factors[r][:, b : b + 1])
+
+    def store(r, b0, b1):
+        cols = slice(WIDE * b0, WIDE * b1)
+        nc.sync.dma_start(out=out_rows[r, :, cols], in_=negs[r][:, cols])
+
+    def finish(r, step):
+        if step == 1:
+            bank_factors(r)
+            for b in range(LEFT_BANKS):
+                scale_left(r, b)
+                if b == 1 or b == LEFT_BANKS - 1:
+                    store(r, 0 if b == 1 else 2, b + 1)
+        elif step - 2 < KEY_CHUNKS - LEFT_BANKS:
+            scale_right(r, LEFT_BANKS + step - 2)
+            if LEFT_BANKS + step - 2 == KEY_CHUNKS - 1:
+                store(r, LEFT_BANKS, KEY_CHUNKS)
 
     for r in range(ROW_TILES):
         scores(r)
-        for b in range(KEY_CHUNKS // 2):
-            drain(r, b)
-        if r > 0:
-            normalise(r - 1)
-        for b in range(KEY_CHUNKS // 2, KEY_CHUNKS):
-            drain(r, b)
-        exponent(r)
-    normalise(ROW_TILES - 1)
+        exponent(r, 0)
+        for b in range(1, KEY_CHUNKS):
+            if r > 0:
+                finish(r - 1, b)
+            exponent(r, b)
+        bank_weights(r)
+    for step in range(1, KEY_CHUNKS):
+        finish(ROW_TILES - 1, step)
 
 
 def tile_visionattention_pa_l_kernel(tc, x, Wq, bq, k, out):

@@ -32,6 +32,7 @@ RUNS = UNITS // 2
 X_LEAD = 6
 X_SPLIT = 256
 GRP_BUFS = 2
+MX_ALIGN = 256
 QBF_BUFS = 3
 ROW_TILES = TOKENS // P
 KEY_CHUNKS = KEYS // WIDE
@@ -50,13 +51,14 @@ def project_queries(tc, keep, psum, pool, x_rows, w_rows, k_rows, bq_cols, k_cod
     x_raws, x_grouped, x_planes = {}, {}, {}
     accs, q_rows, q_grouped = {}, {}, {}
 
-    w_codes = [pool.tile([P, PASSES, P], U32, name="w_codes%d" % r, align_bytes=64) for r in range(W_UNITS)]
-    w_planes = [pool.tile([P, P], U8, name="w_planes%d" % r, align_bytes=64) for r in range(W_UNITS)]
+    w_code_tile = pool.tile([P, W_UNITS, PASSES, P], U32, name="w_codes", align_bytes=MX_ALIGN)
+    w_plane_tile = pool.tile([P, W_UNITS, P], U8, name="w_planes", align_bytes=MX_ALIGN)
+    w_codes = [w_code_tile[:, r] for r in range(W_UNITS)]
+    w_planes = [w_plane_tile[:, r] for r in range(W_UNITS)]
     ident = pool.tile([P, P], F32, name="ident")
     warm = pool.tile([P, 1], F32, name="warm")
     bq_raw = pool.tile([P, GROUPS, PACK], BF16, name="bq_raw")
     bias = pool.tile([P, W_UNITS], F32, name="bias")
-    x_codes[CHUNKS - 1] = pool.tile([P, PASSES, WIDE], U32, name="x_last", align_bytes=64)
 
     def load_unit(u):
         if u >= UNITS:
@@ -125,7 +127,7 @@ def project_queries(tc, keep, psum, pool, x_rows, w_rows, k_rows, bq_cols, k_cod
     def quantize_x(xu):
         i, g = divmod(xu, PASSES)
         if g == 0:
-            x_planes[i] = pool.tile([P, WIDE], U8, name="xp", tag="xp", bufs=3, align_bytes=64)
+            x_planes[i] = pool.tile([P, WIDE], U8, name="xp", tag="xp", bufs=3, align_bytes=MX_ALIGN)
         nc.vector.quantize_mx(
             out=x_codes[i][:, g, :].bitcast(FP8X4),
             scales=plane(x_planes[i], g, slice(0, WIDE)),
@@ -166,8 +168,6 @@ def project_queries(tc, keep, psum, pool, x_rows, w_rows, k_rows, bq_cols, k_cod
 
     def quantize_q(n):
         i, a = divmod(n, GROUPS)
-        if a == 0 and i > 0:
-            q_codes[i] = keep.tile([P, PASSES, WIDE], U32, name="slot%d" % i, tag="slot%d" % i, align_bytes=64)
         nc.vector.quantize_mx(
             out=q_codes[i][:, a, :].bitcast(FP8X4),
             scales=plane(q_planes[i], a, slice(0, WIDE)),
@@ -351,13 +351,15 @@ def tile_visionattention_pa_l_kernel(tc, x, Wq, bq, k, out):
         keep = ctx.enter_context(tc.tile_pool(name="keep", bufs=1))
         psum = ctx.enter_context(tc.psum_pool(name="psum", bufs=4))
 
-        k_codes = [keep.tile([P, PASSES, WIDE], U32, name="k_codes%d" % b, align_bytes=64) for b in range(KEY_CHUNKS)]
-        k_planes = [keep.tile([P, WIDE], U8, name="k_planes%d" % b, align_bytes=64) for b in range(KEY_CHUNKS)]
-        q_planes = [keep.tile([P, WIDE], U8, name="q_planes%d" % i, align_bytes=64) for i in range(CHUNKS)]
-        q_codes = {0: keep.tile([P, PASSES, WIDE], U32, name="slot0", tag="slot0", align_bytes=64)}
-        x_codes = {}
-        for i in range(CHUNKS - 1):
-            x_codes[i] = keep.tile([P, PASSES, WIDE], U32, name="slot%d" % (i + 1), tag="slot%d" % (i + 1), align_bytes=64)
+        k_code_tile = keep.tile([P, KEY_CHUNKS, PASSES, WIDE], U32, name="k_codes", align_bytes=MX_ALIGN)
+        k_plane_tile = keep.tile([P, KEY_CHUNKS, WIDE], U8, name="k_planes", align_bytes=MX_ALIGN)
+        q_plane_tile = keep.tile([P, CHUNKS, WIDE], U8, name="q_planes", align_bytes=MX_ALIGN)
+        slots = keep.tile([P, CHUNKS + 1, PASSES, WIDE], U32, name="slots", align_bytes=MX_ALIGN)
+        k_codes = [k_code_tile[:, b] for b in range(KEY_CHUNKS)]
+        k_planes = [k_plane_tile[:, b] for b in range(KEY_CHUNKS)]
+        q_planes = [q_plane_tile[:, i] for i in range(CHUNKS)]
+        q_codes = [slots[:, i] for i in range(CHUNKS)]
+        x_codes = [slots[:, i + 1] for i in range(CHUNKS)]
 
         with tc.tile_pool(name="first", bufs=1) as first:
             project_queries(tc, keep, psum, first, x_rows, w_rows, k_rows, bq_cols, k_codes, k_planes, x_codes, q_codes, q_planes)

@@ -30,10 +30,11 @@ W_UNITS = C // P
 UNITS = W_UNITS + KEYS // P
 RUNS = UNITS // 2
 X_LEAD = 6
-X_SPLIT = 256
+X_SPLIT = 384
 GRP_BUFS = 2
 MX_ALIGN = 256
-QBF_BUFS = 3
+QBF_BUFS = 2
+HEAD_SPLIT = 256
 ROW_TILES = TOKENS // P
 KEY_CHUNKS = KEYS // WIDE
 LEFT_BANKS = 5
@@ -47,7 +48,7 @@ def project_queries(tc, keep, psum, pool, x_rows, w_rows, k_rows, bq_cols, k_cod
     nc = tc.nc
     inv_sqrt_c = 1.0 / math.sqrt(C)
 
-    raws, banks, turned = {}, {}, {}
+    raws, banks, turned, sorted_units = {}, {}, {}, {}
     x_raws, x_grouped, x_planes = {}, {}, {}
     accs, q_rows, q_grouped = {}, {}, {}
 
@@ -68,6 +69,11 @@ def project_queries(tc, keep, psum, pool, x_rows, w_rows, k_rows, bq_cols, k_cod
         nc.sync.dma_start(out=raw[:], in_=rows)
         raws[u] = raw
 
+    def sort_unit(u):
+        ordered = pool.tile([P, PASSES, 2, P], F32, name="srt", tag="srt", bufs=2)
+        nc.scalar.copy(out=ordered[:], in_=raws[u][:].bitcast(F32).rearrange("p (g w e) -> p g e w", g=PASSES, e=2))
+        sorted_units[u] = ordered
+
     def transpose_run(run):
         for u in (2 * run, 2 * run + 1):
             words = raws[u][:].bitcast(F32)
@@ -77,7 +83,10 @@ def project_queries(tc, keep, psum, pool, x_rows, w_rows, k_rows, bq_cols, k_cod
                 for a in range(2):
                     g = 2 * h + a
                     for e in range(2):
-                        nc.tensor.transpose(view[:, a, e, :], words[:, 256 * g + e : 256 * (g + 1) : 2], ident[:])
+                        if u in sorted_units:
+                            nc.tensor.transpose(view[:, a, e, :], sorted_units[u][:, g, e, :], ident[:])
+                        else:
+                            nc.tensor.transpose(view[:, a, e, :], words[:, 256 * g + e : 256 * (g + 1) : 2], ident[:])
                 banks[(u, h)] = bank
         load_unit(2 * run + 4)
         load_unit(2 * run + 5)
@@ -106,23 +115,24 @@ def project_queries(tc, keep, psum, pool, x_rows, w_rows, k_rows, bq_cols, k_cod
                 in_=turned[u][:, g].rearrange("p r j -> p (r j)"),
             )
 
-    def load_x(xu):
-        if xu >= BLOCKS:
-            return
-        i, g = divmod(xu, PASSES)
-        raw = pool.tile([P, PACK, WIDE], BF16, name="xraw", tag="xraw", bufs=3)
-        nc.sync.dma_start(out=raw[:], in_=x_rows[g, :, :, WIDE * i : WIDE * (i + 1)])
-        x_raws[xu] = raw
+    def load_x(last):
+        for xu in range(len(x_raws), min(last + 1, BLOCKS)):
+            i, g = divmod(xu, PASSES)
+            if xu in (2, 3):
+                raw = pool.tile([P, PACK, WIDE], BF16, name="srt", tag="srt", bufs=2)
+            else:
+                raw = pool.tile([P, PACK, WIDE], BF16, name="xraw", tag="xraw", bufs=2)
+            nc.sync.dma_start(out=raw[:], in_=x_rows[g, :, :, WIDE * i : WIDE * (i + 1)])
+            x_raws[xu] = raw
 
-    def interleave_x(xu, shared):
+    def interleave_x(xu, split):
         grouped = pool.tile([P, WIDE, PACK], BF16, name="grp", tag="grp", bufs=GRP_BUFS, align_bytes=64)
         turned_x = x_raws[xu][:].rearrange("p j n -> p n j")
-        split = X_SPLIT if shared else WIDE
         nc.vector.tensor_copy(out=grouped[:, :split, :], in_=turned_x[:, :split, :])
-        if shared:
+        if split < WIDE:
             nc.scalar.copy(out=grouped[:, split:, :], in_=turned_x[:, split:, :])
         x_grouped[xu] = grouped
-        load_x(xu + 3)
+        load_x(xu + 4 if xu < 2 else max(xu + 2, 5))
 
     def quantize_x(xu):
         i, g = divmod(xu, PASSES)
@@ -174,19 +184,19 @@ def project_queries(tc, keep, psum, pool, x_rows, w_rows, k_rows, bq_cols, k_cod
             in_=q_grouped[n][:].rearrange("p n j -> p (n j)"),
         )
 
-    for xu in range(3):
-        load_x(xu)
+    load_x(2)
     for u in range(4):
         load_unit(u)
     nc.sync.dma_start(out=bq_raw[:], in_=bq_cols)
+    load_x(3)
     nc.vector.memset(warm[:], 0.0)
     nc.scalar.activation(out=warm[:], in_=warm[:], func=ACT.Exp)
     make_identity(nc, ident[:])
 
-    interleave_x(0, True)
-    interleave_x(1, True)
+    interleave_x(0, HEAD_SPLIT)
+    interleave_x(1, HEAD_SPLIT)
     quantize_x(0)
-    interleave_x(2, True)
+    interleave_x(2, HEAD_SPLIT)
     quantize_x(1)
     nc.vector.tensor_scalar(
         out=bias[:], in0=bq_raw[:].rearrange("p a t -> p (a t)"), scalar1=inv_sqrt_c, scalar2=None, op0=ALU.mult
@@ -195,7 +205,7 @@ def project_queries(tc, keep, psum, pool, x_rows, w_rows, k_rows, bq_cols, k_cod
     transpose_run(0)
     copy_run(0)
     quantize_unit(0)
-    interleave_x(3, True)
+    interleave_x(3, HEAD_SPLIT)
     quantize_unit(1)
     quantize_x(3)
 
@@ -206,7 +216,7 @@ def project_queries(tc, keep, psum, pool, x_rows, w_rows, k_rows, bq_cols, k_cod
         evacuate_half(h // 2, h % 2)
         xu = PASSES + h
         if xu < PASSES + X_LEAD:
-            interleave_x(xu, False)
+            interleave_x(xu, WIDE)
         quantize_unit(2 * h + 2)
         if h % 2 == 0 and h >= 2:
             interleave_q(h // 2 - 1)
@@ -223,6 +233,8 @@ def project_queries(tc, keep, psum, pool, x_rows, w_rows, k_rows, bq_cols, k_cod
     run_after = {}
     for j in range(RUNS - first_k_run):
         run_after[GROUPS + 2 * j] = first_k_run + j
+    sort_unit(2 * first_k_run)
+    sort_unit(2 * first_k_run + 1)
     for n in range(GROUPS, BLOCKS):
         project_half(n, 0)
         evacuate_half(n, 0)
@@ -230,13 +242,16 @@ def project_queries(tc, keep, psum, pool, x_rows, w_rows, k_rows, bq_cols, k_cod
         evacuate_half(n, 1)
         xu = n + X_LEAD
         if xu < BLOCKS:
-            interleave_x(xu, n in run_after)
+            interleave_x(xu, WIDE)
         interleave_q(n - 1)
         if xu < BLOCKS:
             quantize_x(xu)
         for u in waiting:
             quantize_unit(u)
         quantize_q(n - 1)
+        if n + 1 in run_after:
+            sort_unit(2 * run_after[n + 1])
+            sort_unit(2 * run_after[n + 1] + 1)
         waiting = []
         if n in run_after:
             transpose_run(run_after[n])

@@ -127,10 +127,15 @@ def project_queries(tc, keep, psum, pool, x_rows, w_rows, k_rows, bq_cols, k_cod
 
     def interleave_x(xu, split):
         grouped = pool.tile([P, WIDE, PACK], BF16, name="grp", tag="grp", bufs=GRP_BUFS, align_bytes=64)
-        turned_x = x_raws[xu][:].rearrange("p j n -> p n j")
-        nc.vector.tensor_copy(out=grouped[:, :split, :], in_=turned_x[:, :split, :])
+        nc.vector.tensor_copy(
+            out=grouped[:, :split, :].rearrange("p (c i) j -> p c j i", i=4),
+            in_=x_raws[xu][:, :, :split].rearrange("p j (c i) -> p c j i", i=4),
+        )
         if split < WIDE:
-            nc.scalar.copy(out=grouped[:, split:, :], in_=turned_x[:, split:, :])
+            nc.scalar.copy(
+                out=grouped[:, split:, :].rearrange("p (c i) j -> p c j i", i=4),
+                in_=x_raws[xu][:, :, split:].rearrange("p j (c i) -> p c j i", i=4),
+            )
         x_grouped[xu] = grouped
         load_x(xu + 4 if xu < 2 else max(xu + 2, 5))
 
@@ -173,7 +178,9 @@ def project_queries(tc, keep, psum, pool, x_rows, w_rows, k_rows, bq_cols, k_cod
 
     def interleave_q(n):
         grouped = pool.tile([P, WIDE, PACK], BF16, name="grp", tag="grp", bufs=GRP_BUFS, align_bytes=64)
-        nc.vector.tensor_copy(out=grouped[:], in_=q_rows[n][:].rearrange("p t n -> p n t"))
+        nc.vector.tensor_copy(
+            out=grouped[:].rearrange("p (c i) t -> p c t i", i=4), in_=q_rows[n][:].rearrange("p t (c i) -> p c t i", i=4)
+        )
         q_grouped[n] = grouped
 
     def quantize_q(n):

import math
from contextlib import ExitStack

import concourse.mybir as mybir
from concourse.masks import make_identity

C = 2048
TOKENS = 4096
KEYS = 4096
FLOPS = 2 * TOKENS * C * C + 2 * TOKENS * KEYS * C

F32 = mybir.dt.float32
BF16 = mybir.dt.bfloat16
U32 = mybir.dt.uint32
U8 = mybir.dt.uint8
FP8X4 = mybir.dt.float8_e4m3fn_x4
ALU = mybir.AluOpType
ACT = mybir.ActivationFunctionType
AX = mybir.AxisListType

P = 128
PACK = 4
PASSES = C // (P * PACK)
WIDE = 512

CHUNKS = TOKENS // WIDE
GROUPS = C // WIDE
BLOCKS = CHUNKS * GROUPS
W_UNITS = C // P
UNITS = W_UNITS + KEYS // P
RUNS = UNITS // 2
X_LEAD = 6
X_SPLIT = 384
GRP_BUFS = 2
MX_ALIGN = 256
QBF_BUFS = 2
HEAD_SPLIT = 256
ROW_TILES = TOKENS // P
KEY_CHUNKS = KEYS // WIDE
LEFT_BANKS = 5


def plane(tile_ap, g, cols):
    return tile_ap[PACK * g : P, cols]


def project_queries(tc, keep, psum, pool, x_rows, w_rows, k_rows, bq_cols, k_codes, k_planes, x_codes, q_codes, q_planes):
    nc = tc.nc
    inv_sqrt_c = 1.0 / math.sqrt(C)

    raws, banks, turned, sorted_units = {}, {}, {}, {}
    x_raws, x_grouped, x_planes = {}, {}, {}
    accs, q_rows, q_grouped = {}, {}, {}

    w_code_tile = pool.tile([P, W_UNITS, PASSES, P], U32, name="w_codes", align_bytes=MX_ALIGN)
    w_plane_tile = pool.tile([P, W_UNITS, P], U8, name="w_planes", align_bytes=MX_ALIGN)
    w_codes = [w_code_tile[:, r] for r in range(W_UNITS)]
    w_planes = [w_plane_tile[:, r] for r in range(W_UNITS)]
    ident = pool.tile([P, P], F32, name="ident")
    warm = pool.tile([P, 1], F32, name="warm")
    bq_raw = pool.tile([P, GROUPS, PACK], BF16, name="bq_raw")
    bias = pool.tile([P, W_UNITS], F32, name="bias")

    def load_unit(u):
        if u >= UNITS:
            return
        raw = pool.tile([P, C], BF16, name="raw", tag="raw", bufs=4)
        rows = w_rows[u // PACK, u % PACK] if u < W_UNITS else k_rows[u - W_UNITS]
        nc.sync.dma_start(out=raw[:], in_=rows)
        raws[u] = raw

    def sort_unit(u):
        ordered = pool.tile([P, PASSES, 2, P], F32, name="srt", tag="srt", bufs=2)
        nc.scalar.copy(out=ordered[:], in_=raws[u][:].bitcast(F32).rearrange("p (g w e) -> p g e w", g=PASSES, e=2))
        sorted_units[u] = ordered

    def transpose_run(run):
        for u in (2 * run, 2 * run + 1):
            words = raws[u][:].bitcast(F32)
            for h in range(2):
                bank = psum.tile([P, WIDE], F32, name="tr", tag="tr")
                view = bank[:].rearrange("p (a e r) -> p a e r", a=2, e=2)
                for a in range(2):
                    g = 2 * h + a
                    for e in range(2):
                        if u in sorted_units:
                            nc.tensor.transpose(view[:, a, e, :], sorted_units[u][:, g, e, :], ident[:])
                        else:
                            nc.tensor.transpose(view[:, a, e, :], words[:, 256 * g + e : 256 * (g + 1) : 2], ident[:])
                banks[(u, h)] = bank
        load_unit(2 * run + 4)
        load_unit(2 * run + 5)

    def copy_run(run):
        for u in (2 * run, 2 * run + 1):
            grouped = pool.tile([P, PASSES, P, PACK], BF16, name="kg", tag="kg", bufs=2, align_bytes=64)
            for h in range(2):
                nc.scalar.copy(
                    out=grouped[:].bitcast(F32)[:, 2 * h : 2 * h + 2],
                    in_=banks[(u, h)][:].rearrange("p (a e r) -> p a r e", a=2, e=2),
                )
            turned[u] = grouped

    def quantize_unit(u):
        if u < W_UNITS:
            codes, planes, c0 = w_codes[u], w_planes[u], 0
        else:
            v = u - W_UNITS
            codes, planes, c0 = k_codes[v // PACK], k_planes[v // PACK], P * (v % PACK)
        cols = slice(c0, c0 + P)
        for g in range(PASSES):
            nc.vector.quantize_mx(
                out=codes[:, g, cols].bitcast(FP8X4),
                scales=plane(planes, g, cols),
                in_=turned[u][:, g].rearrange("p r j -> p (r j)"),
            )

    def load_x(last):
        for xu in range(len(x_raws), min(last + 1, BLOCKS)):
            i, g = divmod(xu, PASSES)
            if xu in (2, 3):
                raw = pool.tile([P, PACK, WIDE], BF16, name="srt", tag="srt", bufs=2)
            else:
                raw = pool.tile([P, PACK, WIDE], BF16, name="xraw", tag="xraw", bufs=2)
            nc.sync.dma_start(out=raw[:], in_=x_rows[g, :, :, WIDE * i : WIDE * (i + 1)])
            x_raws[xu] = raw

    def interleave_x(xu, split):
        grouped = pool.tile([P, WIDE, PACK], BF16, name="grp", tag="grp", bufs=GRP_BUFS, align_bytes=64)
        nc.vector.tensor_copy(
            out=grouped[:, :split, :].rearrange("p (c i) j -> p c j i", i=4),
            in_=x_raws[xu][:, :, :split].rearrange("p j (c i) -> p c j i", i=4),
        )
        if split < WIDE:
            nc.scalar.copy(
                out=grouped[:, split:, :].rearrange("p (c i) j -> p c j i", i=4),
                in_=x_raws[xu][:, :, split:].rearrange("p j (c i) -> p c j i", i=4),
            )
        x_grouped[xu] = grouped
        load_x(xu + 4 if xu < 2 else max(xu + 2, 5))

    def quantize_x(xu):
        i, g = divmod(xu, PASSES)
        if g == 0:
            x_planes[i] = pool.tile([P, WIDE], U8, name="xp", tag="xp", bufs=3, align_bytes=MX_ALIGN)
        nc.vector.quantize_mx(
            out=x_codes[i][:, g, :].bitcast(FP8X4),
            scales=plane(x_planes[i], g, slice(0, WIDE)),
            in_=x_grouped[xu][:].rearrange("p n j -> p (n j)"),
        )

    def project_half(n, half):
        i, a = divmod(n, GROUPS)
        for t in (2 * half, 2 * half + 1):
            r = PACK * a + t
            acc = psum.tile([P, WIDE], F32, name="acc", tag="acc")
            for g in range(PASSES):
                nc.tensor.matmul_mx(
                    out=acc[:],
                    lhsT=w_codes[r][:, g, :].bitcast(FP8X4),
                    lhsT_scale=plane(w_planes[r], g, slice(0, P)),
                    rhs=x_codes[i][:, g, :].bitcast(FP8X4),
                    rhs_scale=plane(x_planes[i], g, slice(0, WIDE)),
                    start=(g == 0),
                    stop=(g == PASSES - 1),
                )
            accs[(n, t)] = acc

    def evacuate_half(n, half):
        a = n % GROUPS
        if half == 0:
            q_rows[n] = pool.tile([P, PACK, WIDE], BF16, name="qbf", tag="qbf", bufs=QBF_BUFS)
        for t in (2 * half, 2 * half + 1):
            r = PACK * a + t
            nc.scalar.activation(
                out=q_rows[n][:, t, :], in_=accs[(n, t)][:], func=ACT.Identity, bias=bias[:, r : r + 1], scale=inv_sqrt_c
            )

    def interleave_q(n):
        grouped = pool.tile([P, WIDE, PACK], BF16, name="grp", tag="grp", bufs=GRP_BUFS, align_bytes=64)
        nc.vector.tensor_copy(
            out=grouped[:].rearrange("p (c i) t -> p c t i", i=4), in_=q_rows[n][:].rearrange("p t (c i) -> p c t i", i=4)
        )
        q_grouped[n] = grouped

    def quantize_q(n):
        i, a = divmod(n, GROUPS)
        nc.vector.quantize_mx(
            out=q_codes[i][:, a, :].bitcast(FP8X4),
            scales=plane(q_planes[i], a, slice(0, WIDE)),
            in_=q_grouped[n][:].rearrange("p n j -> p (n j)"),
        )

    load_x(2)
    for u in range(4):
        load_unit(u)
    nc.sync.dma_start(out=bq_raw[:], in_=bq_cols)
    load_x(3)
    nc.vector.memset(warm[:], 0.0)
    nc.scalar.activation(out=warm[:], in_=warm[:], func=ACT.Exp)
    make_identity(nc, ident[:])

    interleave_x(0, HEAD_SPLIT)
    interleave_x(1, HEAD_SPLIT)
    quantize_x(0)
    interleave_x(2, HEAD_SPLIT)
    quantize_x(1)
    nc.vector.tensor_scalar(
        out=bias[:], in0=bq_raw[:].rearrange("p a t -> p (a t)"), scalar1=inv_sqrt_c, scalar2=None, op0=ALU.mult
    )
    quantize_x(2)
    transpose_run(0)
    copy_run(0)
    quantize_unit(0)
    interleave_x(3, HEAD_SPLIT)
    quantize_unit(1)
    quantize_x(3)

    for h in range(2 * GROUPS):
        transpose_run(h + 1)
        copy_run(h + 1)
        project_half(h // 2, h % 2)
        evacuate_half(h // 2, h % 2)
        xu = PASSES + h
        if xu < PASSES + X_LEAD:
            interleave_x(xu, WIDE)
        quantize_unit(2 * h + 2)
        if h % 2 == 0 and h >= 2:
            interleave_q(h // 2 - 1)
        quantize_unit(2 * h + 3)
        if xu < PASSES + X_LEAD:
            quantize_x(xu)
        if h % 2 == 0 and h >= 2:
            quantize_q(h // 2 - 1)

    transpose_run(2 * GROUPS + 1)
    copy_run(2 * GROUPS + 1)
    waiting = [4 * GROUPS + 2, 4 * GROUPS + 3]
    first_k_run = 2 * GROUPS + 2
    run_after = {}
    for j in range(RUNS - first_k_run):
        run_after[GROUPS + 2 * j] = first_k_run + j
    sort_unit(2 * first_k_run)
    sort_unit(2 * first_k_run + 1)
    for n in range(GROUPS, BLOCKS):
        project_half(n, 0)
        evacuate_half(n, 0)
        project_half(n, 1)
        evacuate_half(n, 1)
        xu = n + X_LEAD
        if xu < BLOCKS:
            interleave_x(xu, WIDE)
        interleave_q(n - 1)
        if xu < BLOCKS:
            quantize_x(xu)
        for u in waiting:
            quantize_unit(u)
        quantize_q(n - 1)
        if n + 1 in run_after:
            sort_unit(2 * run_after[n + 1])
            sort_unit(2 * run_after[n + 1] + 1)
        waiting = []
        if n in run_after:
            transpose_run(run_after[n])
            copy_run(run_after[n])
            waiting = [2 * run_after[n], 2 * run_after[n] + 1]
    interleave_q(BLOCKS - 1)
    for u in waiting:
        quantize_unit(u)
    quantize_q(BLOCKS - 1)


def attention_rows(tc, psum, pool, q_codes, q_planes, k_codes, k_planes, out_rows):
    nc = tc.nc
    banks, negs, lows, sums, shifts, weights, factors = {}, {}, {}, {}, {}, {}, {}

    def bank_cols(b):
        return slice(WIDE * b, WIDE * (b + 1))

    def scores(r):
        i, s = divmod(r, WIDE // P)
        cols = slice(P * s, P * (s + 1))
        for b in range(KEY_CHUNKS):
            bank = psum.tile([P, WIDE], F32, name="sc", tag=("acc", "tr")[b % 2])
            for g in range(PASSES):
                nc.tensor.matmul_mx(
                    out=bank[:],
                    lhsT=q_codes[i][:, g, cols].bitcast(FP8X4),
                    lhsT_scale=plane(q_planes[i], g, cols),
                    rhs=k_codes[b][:, g, :].bitcast(FP8X4),
                    rhs_scale=plane(k_planes[b], g, slice(0, WIDE)),
                    start=(g == 0),
                    stop=(g == PASSES - 1),
                )
            banks[(r, b)] = bank

    def exponent(r, b):
        if b == 0:
            negs[r] = pool.tile([P, KEYS], F32, name="neg", tag="neg", bufs=4)
            lows[r] = pool.tile([P, KEY_CHUNKS], F32, name="low", tag="low", bufs=3)
            sums[r] = pool.tile([P, KEY_CHUNKS], F32, name="sums", tag="sums", bufs=3)
        part = negs[r][:, bank_cols(b)]
        nc.vector.tensor_scalar(
            out=part, in0=banks[(r, b)][:], scalar1=-1.0, scalar2=None, op0=ALU.mult, op1=ALU.min, accum_out=lows[r][:, b : b + 1]
        )
        nc.scalar.activation(
            out=part, in_=part, func=ACT.Exp, bias=lows[r][:, b : b + 1], scale=-1.0, accum_out=sums[r][:, b : b + 1]
        )

    def bank_weights(r):
        shifts[r] = pool.tile([P, 1], F32, name="shift", tag="shift", bufs=3)
        weights[r] = pool.tile([P, KEY_CHUNKS], F32, name="weight", tag="weight", bufs=3)
        nc.vector.tensor_reduce(out=shifts[r][:], in_=lows[r][:], axis=AX.X, op=ALU.min)
        nc.scalar.activation(out=weights[r][:], in_=lows[r][:], func=ACT.Exp, bias=shifts[r][:, 0:1], scale=-1.0)

    def bank_factors(r):
        weighted = pool.tile([P, KEY_CHUNKS], F32, name="weighted", tag="weighted", bufs=3)
        total = pool.tile([P, 1], F32, name="total", tag="total", bufs=3)
        inv = pool.tile([P, 1], F32, name="inv", tag="inv", bufs=3)
        factors[r] = pool.tile([P, KEY_CHUNKS], F32, name="factor", tag="factor", bufs=3)
        nc.vector.scalar_tensor_tensor(
            out=weighted[:], in0=weights[r][:], scalar=1.0, in1=sums[r][:], op0=ALU.mult, op1=ALU.mult, accum_out=total[:, 0:1]
        )
        nc.vector.reciprocal(out=inv[:], in_=total[:])
        nc.vector.tensor_scalar(out=factors[r][:], in0=weights[r][:], scalar1=inv[:, 0:1], scalar2=None, op0=ALU.mult)

    def scale_left(r, b):
        engine = nc.vector if r == ROW_TILES - 1 else nc.gpsimd
        part = negs[r][:, bank_cols(b)]
        engine.tensor_scalar(out=part, in0=part, scalar1=factors[r][:, b : b + 1], scalar2=0.0, op0=ALU.mult, op1=ALU.add)

    def scale_right(r, b):
        part = negs[r][:, bank_cols(b)]
        nc.scalar.activation(out=part, in_=part, func=ACT.Copy, scale=factors[r][:, b : b + 1])

    def store(r, b0, b1):
        cols = slice(WIDE * b0, WIDE * b1)
        nc.sync.dma_start(out=out_rows[r, :, cols], in_=negs[r][:, cols])

    def finish(r, step):
        if step == 1:
            bank_factors(r)
            for b in range(LEFT_BANKS):
                scale_left(r, b)
                if b == 1 or b == LEFT_BANKS - 1:
                    store(r, 0 if b == 1 else 2, b + 1)
        elif step - 2 < KEY_CHUNKS - LEFT_BANKS:
            scale_right(r, LEFT_BANKS + step - 2)
            if LEFT_BANKS + step - 2 == KEY_CHUNKS - 1:
                store(r, LEFT_BANKS, KEY_CHUNKS)

    for r in range(ROW_TILES):
        scores(r)
        exponent(r, 0)
        for b in range(1, KEY_CHUNKS):
            if r > 0:
                finish(r - 1, b)
            exponent(r, b)
        bank_weights(r)
    for step in range(1, KEY_CHUNKS):
        finish(ROW_TILES - 1, step)


def tile_visionattention_pa_l_kernel(tc, x, Wq, bq, k, out):
    x_rows = x[0].rearrange("(g p j) h w -> g p j (h w)", p=P, j=PACK)
    w_rows = Wq.rearrange("(a m t) c -> a t m c", m=P, t=PACK)
    k_rows = k[0].rearrange("(u p) c -> u p c", p=P)
    bq_cols = bq.rearrange("(a m t) -> m a t", m=P, t=PACK)
    out_rows = out[0].rearrange("(r p) m -> r p m", p=P)

    with ExitStack() as ctx:
        ctx.enter_context(tc.manual_schedule())
        keep = ctx.enter_context(tc.tile_pool(name="keep", bufs=1))
        psum = ctx.enter_context(tc.psum_pool(name="psum", bufs=4))

        k_code_tile = keep.tile([P, KEY_CHUNKS, PASSES, WIDE], U32, name="k_codes", align_bytes=MX_ALIGN)
        k_plane_tile = keep.tile([P, KEY_CHUNKS, WIDE], U8, name="k_planes", align_bytes=MX_ALIGN)
        q_plane_tile = keep.tile([P, CHUNKS, WIDE], U8, name="q_planes", align_bytes=MX_ALIGN)
        slots = keep.tile([P, CHUNKS + 1, PASSES, WIDE], U32, name="slots", align_bytes=MX_ALIGN)
        k_codes = [k_code_tile[:, b] for b in range(KEY_CHUNKS)]
        k_planes = [k_plane_tile[:, b] for b in range(KEY_CHUNKS)]
        q_planes = [q_plane_tile[:, i] for i in range(CHUNKS)]
        q_codes = [slots[:, i] for i in range(CHUNKS)]
        x_codes = [slots[:, i + 1] for i in range(CHUNKS)]

        with tc.tile_pool(name="first", bufs=1) as first:
            project_queries(tc, keep, psum, first, x_rows, w_rows, k_rows, bq_cols, k_codes, k_planes, x_codes, q_codes, q_planes)
        with tc.tile_pool(name="second", bufs=1) as second:
            attention_rows(tc, psum, second, q_codes, q_planes, k_codes, k_planes, out_rows)
